import numpy as np
import ml_dtypes


def mxq(x, axis, fmt="e4m3"):
    dtype, down = {"e4m3": (ml_dtypes.float8_e4m3fn, 7), "e5m2": (ml_dtypes.float8_e5m2, 14)}[fmt]
    v = np.moveaxis(np.asarray(x, np.float32).astype(ml_dtypes.bfloat16).astype(np.float64), axis, -1)
    blocks = v.reshape(v.shape[:-1] + (-1, 32))
    amax = np.abs(blocks).max(-1, keepdims=True)
    byte = np.maximum(np.where(amax > 0, np.frexp(amax)[1] - 1 + 127, 0) - down, 1)
    scale = np.exp2(byte - 127.0)
    codes = (blocks / scale).astype(np.float32).astype(dtype).astype(np.float64)
    return np.moveaxis((codes * scale).reshape(v.shape), -1, axis)


WIDE = False


def mx_kscale(k):
    if not WIDE:
        return np.ones(k)
    levels = np.array([10, -10, 5, -5, 0])
    a = np.random.permutation(np.resize(levels, k // 512 * 4)).reshape(k // 512, 4)
    idx = np.arange(k)
    return np.exp2(a[idx // 512, idx % 128 // 32])


BF16 = ml_dtypes.bfloat16


def bf(x):
    return np.asarray(x, np.float32).astype(BF16)


def f64(x):
    return np.asarray(x).astype(np.float64)


B, F, G, N, L = 256, 512, 16, 100, 7
S2 = (L + 1) ** 2


def setup_inputs():
    s = mx_kscale(F)
    return {"x": bf(np.random.standard_normal((B, F, S2)) * s[None, :, None]),
            "psi": bf(np.random.standard_normal((G, F, S2)) / s[None, :, None])}


def reference(x, psi):
    xq = mxq(f64(x), 1, "e4m3")
    pq = mxq(f64(psi), 1, "e4m3")
    scale = 1.0 / np.sqrt(F)
    outs = []
    for l in range(L + 1):
        s, d = l * l, 2 * l + 1
        a = xq[:, :, s:s + d].transpose(0, 2, 1).reshape(B * d, F)
        p = pq[:, :, s:s + d].transpose(1, 0, 2).reshape(F, G * d)
        o = scale * (a @ p)
        outs.append(o.reshape(B, d, G, d).transpose(2, 0, 1, 3).reshape(G, B, d * d))
    return np.concatenate(outs, axis=-1)

@@ -1,0 +1,215 @@
+import math
+from contextlib import ExitStack
+
+import concourse.bass as bass
+import concourse.mybir as mybir
+import concourse.tile as tile
+
+FP8X4 = mybir.dt.float8_e4m3fn_x4
+BF16 = mybir.dt.bfloat16
+F32 = mybir.dt.float32
+U32 = mybir.dt.uint32
+U8 = mybir.dt.uint8
+
+P = 128
+PACK = 4
+BATCH, FEAT, GOUT, COEF = 256, 512, 16, 64
+NDEG = 8
+OUTW = 680
+FLOPS = 2 * FEAT * BATCH * GOUT * OUTW
+SCALE = 1.0 / math.sqrt(FEAT)
+
+SUB = 16
+NSUB = BATCH // SUB
+CHUNK = 64
+SUBS_PER_CHUNK = CHUNK // SUB
+CBLK = 16
+NCBLK = COEF // CBLK
+GH = 8
+BANK_C = 4
+NBANK = COEF // BANK_C
+
+DEGREE = [l for l in range(NDEG) for u in range(2 * l + 1)]
+ORDER_U = [u for l in range(NDEG) for u in range(2 * l + 1)]
+BLOCK0 = [sum((2 * k + 1) ** 2 for k in range(l)) for l in range(NDEG)]
+WINDOW = [l if l < 4 else 7 - l for l in range(NDEG)]
+WOFF = [GH * (2 * (7 - l) + 1) if l < 4 else 0 for l in range(NDEG)]
+
+
+def degree_runs(i):
+    runs = []
+    for t in range(BANK_C):
+        l = DEGREE[BANK_C * i + t]
+        if runs and runs[-1][0] == l:
+            runs[-1][2] += 1
+        else:
+            runs.append([l, t, 1])
+    return runs
+
+
+def tile_s2conv_pa_t_kernel(tc, x, psi, out):
+    nc = tc.nc
+    xv = x.rearrange("b (p j) c -> p b (j c)", j=PACK)
+    pv = psi.rearrange("g (p j) c -> p g (j c)", j=PACK)
+
+    with ExitStack() as ctx:
+        raw_pool = ctx.enter_context(tc.tile_pool(name="raw", bufs=4))
+        grp_pool = ctx.enter_context(tc.tile_pool(name="grp", bufs=6))
+        cod_pool = ctx.enter_context(tc.tile_pool(name="cod", bufs=6))
+        stg_pool = ctx.enter_context(tc.tile_pool(name="stg", bufs=4))
+        psi_pool = ctx.enter_context(tc.tile_pool(name="psi", bufs=1))
+        psum = ctx.enter_context(tc.psum_pool(name="psum", bufs=8))
+        ctx.enter_context(tc.manual_schedule())
+
+        raw = {}
+        grp = {}
+        cod = {}
+        scl = {}
+        stg = {}
+
+        def load(s):
+            t = raw_pool.tile([P, SUB * PACK, COEF], BF16, name="raw%d" % s, tag="raw")
+            raw[s] = t
+            nc.sync.dma_start(
+                out=t[:].rearrange("p (b j) c -> p b (j c)", j=PACK),
+                in_=xv[:, SUB * s : SUB * (s + 1), :],
+            )
+
+        def copy_on(vector, dst, src):
+            if vector:
+                nc.vector.tensor_copy(out=dst, in_=src)
+            else:
+                nc.scalar.copy(out=dst, in_=src)
+
+        def regroup(s, q, vector):
+            k = s // SUBS_PER_CHUNK
+            part = s % SUBS_PER_CHUNK
+            if part == 0:
+                grp[(k, q)] = grp_pool.tile(
+                    [P, CBLK, CHUNK * PACK], BF16, name="grp%d_%d" % (k, q), tag="grp", align_bytes=64
+                )
+            width = SUB * PACK
+            dst = grp[(k, q)][:, :, width * part : width * (part + 1)]
+            src = raw[s][:, :, CBLK * q : CBLK * (q + 1)]
+            copy_on(
+                vector,
+                dst.rearrange("p (a i) r -> p a r i", i=4),
+                src.rearrange("p r (a i) -> p a r i", i=4),
+            )
+
+        def quantise(k, q):
+            h = k // 2
+            half = k % 2
+            if half == 0:
+                cod[(h, q)] = cod_pool.tile(
+                    [P, CBLK, P], U32, name="cod%d_%d" % (h, q), tag="cod", align_bytes=64
+                )
+                scl[(h, q)] = cod_pool.tile(
+                    [P, CBLK, P], U8, name="scl%d_%d" % (h, q), tag="scl", align_bytes=64
+                )
+            cols = slice(CHUNK * half, CHUNK * (half + 1))
+            for c in range(CBLK):
+                nc.vector.quantize_mx(
+                    out=cod[(h, q)][:, c, cols].bitcast(FP8X4),
+                    scales=scl[(h, q)][:, c, cols],
+                    in_=grp[(k, q)][:, c, :],
+                )
+
+        def bank(h, y, i, vector):
+            if (h, y) not in stg:
+                stg[(h, y)] = stg_pool.tile([P, GH, OUTW], F32, name="stg%d_%d" % (h, y), tag="stg")
+            acc = psum.tile([P, BANK_C, P], F32, name="acc%d_%d_%d" % (h, y, i), tag="acc")
+            q = i // (NBANK // NCBLK)
+            for t in range(BANK_C):
+                c = BANK_C * i + t
+                w = P * (4 * y + WINDOW[DEGREE[c]])
+                nc.tensor.matmul_mx(
+                    out=acc[:, t, :],
+                    lhsT=cod[(h, q)][:, c % CBLK, :].bitcast(FP8X4),
+                    lhsT_scale=scl[(h, q)][:, c % CBLK, :],
+                    rhs=pcod[:, w : w + P].bitcast(FP8X4),
+                    rhs_scale=pscl[:, w : w + P],
+                    start=True,
+                    stop=True,
+                )
+            for l, t0, n in degree_runs(i):
+                d = 2 * l + 1
+                col = BLOCK0[l] + ORDER_U[BANK_C * i + t0] * d
+                src = acc[:, t0 : t0 + n, WOFF[l] : WOFF[l] + GH * d].rearrange(
+                    "p n (g m) -> p g n m", g=GH
+                )
+                dst = stg[(h, y)][:, :, col : col + n * d].rearrange("p g (n m) -> p g n m", n=n)
+                if vector:
+                    nc.vector.tensor_scalar_mul(out=dst, in0=src, scalar1=SCALE)
+                else:
+                    nc.scalar.mul(out=dst, in_=src, mul=SCALE)
+
+        def store(h, y):
+            nc.sync.dma_start(
+                out=out[GH * y : GH * (y + 1), P * h : P * (h + 1), :].rearrange("g b n -> b g n"),
+                in_=stg[(h, y)][:],
+            )
+
+        praw = raw_pool.tile([P, GOUT, PACK, COEF], BF16, name="praw", tag="raw")
+        nc.sync.dma_start(out=praw[:].rearrange("p g j c -> p g (j c)"), in_=pv)
+        for s in range(3):
+            load(s)
+        pgrp = grp_pool.tile([P, 2 * 4 * P, PACK], BF16, name="pgrp", tag="grp", align_bytes=64)
+        pcod = psi_pool.tile([P, 2 * 4 * P], U32, name="pcod", align_bytes=64)
+        pscl = psi_pool.tile([P, 2 * 4 * P], U8, name="pscl", align_bytes=64)
+        for y in range(2):
+            for l in range(NDEG):
+                d = 2 * l + 1
+                c0 = P * (4 * y + WINDOW[l]) + WOFF[l]
+                copy_on(
+                    y == 0,
+                    pgrp[:, c0 : c0 + GH * d, :].rearrange("p (g m) j -> p g m j", g=GH),
+                    praw[:, GH * y : GH * (y + 1), :, l * l : l * l + d].rearrange("p g j m -> p g m j"),
+                )
+
+        todo = [(0, y, i) for y in range(2) for i in range(NBANK)]
+        done = 0
+        for s in range(NSUB):
+            if s + 3 < NSUB:
+                load(s + 3)
+            k = s // SUBS_PER_CHUNK
+            part = s % SUBS_PER_CHUNK
+            nvec = 2 if s < 8 else 3
+            for q in range(NCBLK):
+                regroup(s, q, q < nvec)
+            if s >= 8:
+                for n in range(4 if s < 10 else 5):
+                    if done < len(todo):
+                        h, y, i = todo[done]
+                        bank(h, y, i, False)
+                        done += 1
+            if s == 0:
+                nc.vector.quantize_mx(
+                    out=pcod[:].bitcast(FP8X4),
+                    scales=pscl[:],
+                    in_=pgrp[:].rearrange("p n j -> p (n j)"),
+                )
+            if s == NSUB - 1:
+                for q in range(NCBLK):
+                    quantise(k, q)
+            elif part == 3:
+                quantise(k, 0)
+                quantise(k, 1)
+            elif part == 0 and k > 0:
+                quantise(k - 1, 2)
+            elif part == 1 and k > 0:
+                quantise(k - 1, 3)
+        for h, y, i in todo[done:]:
+            bank(h, y, i, False)
+        store(0, 0)
+        store(0, 1)
+        for i in range(NBANK):
+            bank(1, 0, i, i >= 14)
+        store(1, 0)
+        vlist = list(range(5, 14))
+        slist = [0, 1, 2, 3, 4, 14, 15]
+        for n in range(len(vlist)):
+            bank(1, 1, vlist[n], True)
+            if n < len(slist):
+                bank(1, 1, slist[n], False)
+        store(1, 1)

@@ -19,6 +19,7 @@ OUTW = 680
 FLOPS = 2 * FEAT * BATCH * GOUT * OUTW
 SCALE = 1.0 / math.sqrt(FEAT)
 
+RUNS = 4
 SUB = 16
 NSUB = BATCH // SUB
 CHUNK = 64
@@ -70,10 +71,12 @@ def tile_s2conv_pa_t_kernel(tc, x, psi, out):
         def load(s):
             t = raw_pool.tile([P, SUB * PACK, COEF], BF16, name="raw%d" % s, tag="raw")
             raw[s] = t
-            nc.sync.dma_start(
-                out=t[:].rearrange("p (b j) c -> p b (j c)", j=PACK),
-                in_=xv[:, SUB * s : SUB * (s + 1), :],
-            )
+            tv = t[:].rearrange("p (b j) c -> p b (j c)", j=PACK)
+            for b0 in range(0, SUB, RUNS):
+                nc.sync.dma_start(
+                    out=tv[:, b0 : b0 + RUNS, :],
+                    in_=xv[:, SUB * s + b0 : SUB * s + b0 + RUNS, :],
+                )
 
         def copy_on(vector, dst, src):
             if vector:
@@ -145,13 +148,16 @@ def tile_s2conv_pa_t_kernel(tc, x, psi, out):
                     nc.scalar.mul(out=dst, in_=src, mul=SCALE)
 
         def store(h, y):
-            nc.sync.dma_start(
-                out=out[GH * y : GH * (y + 1), P * h : P * (h + 1), :].rearrange("g b n -> b g n"),
-                in_=stg[(h, y)][:],
-            )
+            for g0 in range(0, GH, RUNS):
+                nc.sync.dma_start(
+                    out=out[GH * y + g0 : GH * y + g0 + RUNS, P * h : P * (h + 1), :].rearrange("g b n -> b g n"),
+                    in_=stg[(h, y)][:, g0 : g0 + RUNS, :],
+                )
 
         praw = raw_pool.tile([P, GOUT, PACK, COEF], BF16, name="praw", tag="raw")
-        nc.sync.dma_start(out=praw[:].rearrange("p g j c -> p g (j c)"), in_=pv)
+        pt = praw[:].rearrange("p g j c -> p g (j c)")
+        for g0 in range(0, GOUT, RUNS):
+            nc.sync.dma_start(out=pt[:, g0 : g0 + RUNS, :], in_=pv[:, g0 : g0 + RUNS, :])
         for s in range(3):
             load(s)
         pgrp = grp_pool.tile([P, 2 * 4 * P, PACK], BF16, name="pgrp", tag="grp", align_bytes=64)

@@ -19,7 +19,6 @@ OUTW = 680
 FLOPS = 2 * FEAT * BATCH * GOUT * OUTW
 SCALE = 1.0 / math.sqrt(FEAT)
 
-RUNS = 4
 SUB = 16
 NSUB = BATCH // SUB
 CHUNK = 64
@@ -71,12 +70,10 @@ def tile_s2conv_pa_t_kernel(tc, x, psi, out):
         def load(s):
             t = raw_pool.tile([P, SUB * PACK, COEF], BF16, name="raw%d" % s, tag="raw")
             raw[s] = t
-            tv = t[:].rearrange("p (b j) c -> p b (j c)", j=PACK)
-            for b0 in range(0, SUB, RUNS):
-                nc.sync.dma_start(
-                    out=tv[:, b0 : b0 + RUNS, :],
-                    in_=xv[:, SUB * s + b0 : SUB * s + b0 + RUNS, :],
-                )
+            nc.sync.dma_start(
+                out=t[:].rearrange("p (b j) c -> p b (j c)", j=PACK),
+                in_=xv[:, SUB * s : SUB * (s + 1), :],
+            )
 
         def copy_on(vector, dst, src):
             if vector:
@@ -96,8 +93,8 @@ def tile_s2conv_pa_t_kernel(tc, x, psi, out):
             src = raw[s][:, :, CBLK * q : CBLK * (q + 1)]
             copy_on(
                 vector,
-                dst.rearrange("p (a i) r -> p a r i", i=4),
-                src.rearrange("p r (a i) -> p a r i", i=4),
+                dst.rearrange("p (a i) r -> p a r i", i=2),
+                src.rearrange("p r (a i) -> p a r i", i=2),
             )
 
         def quantise(k, q):
@@ -148,16 +145,13 @@ def tile_s2conv_pa_t_kernel(tc, x, psi, out):
                     nc.scalar.mul(out=dst, in_=src, mul=SCALE)
 
         def store(h, y):
-            for g0 in range(0, GH, RUNS):
-                nc.sync.dma_start(
-                    out=out[GH * y + g0 : GH * y + g0 + RUNS, P * h : P * (h + 1), :].rearrange("g b n -> b g n"),
-                    in_=stg[(h, y)][:, g0 : g0 + RUNS, :],
-                )
+            nc.sync.dma_start(
+                out=out[GH * y : GH * (y + 1), P * h : P * (h + 1), :].rearrange("g b n -> b g n"),
+                in_=stg[(h, y)][:],
+            )
 
         praw = raw_pool.tile([P, GOUT, PACK, COEF], BF16, name="praw", tag="raw")
-        pt = praw[:].rearrange("p g j c -> p g (j c)")
-        for g0 in range(0, GOUT, RUNS):
-            nc.sync.dma_start(out=pt[:, g0 : g0 + RUNS, :], in_=pv[:, g0 : g0 + RUNS, :])
+        nc.sync.dma_start(out=praw[:].rearrange("p g j c -> p g (j c)"), in_=pv)
         for s in range(3):
             load(s)
         pgrp = grp_pool.tile([P, 2 * 4 * P, PACK], BF16, name="pgrp", tag="grp", align_bytes=64)

@@ -19,6 +19,7 @@ OUTW = 680
 FLOPS = 2 * FEAT * BATCH * GOUT * OUTW
 SCALE = 1.0 / math.sqrt(FEAT)
 
+RUNS = 4
 SUB = 16
 NSUB = BATCH // SUB
 CHUNK = 64
@@ -70,10 +71,13 @@ def tile_s2conv_pa_t_kernel(tc, x, psi, out):
         def load(s):
             t = raw_pool.tile([P, SUB * PACK, COEF], BF16, name="raw%d" % s, tag="raw")
             raw[s] = t
-            nc.sync.dma_start(
-                out=t[:].rearrange("p (b j) c -> p b (j c)", j=PACK),
-                in_=xv[:, SUB * s : SUB * (s + 1), :],
-            )
+            tv = t[:].rearrange("p (b j) c -> p b (j c)", j=PACK)
+            for b0 in range(0, SUB, RUNS):
+                queue = nc.sync if (b0 // RUNS) % 2 == 0 else nc.scalar
+                queue.dma_start(
+                    out=tv[:, b0 : b0 + RUNS, :],
+                    in_=xv[:, SUB * s + b0 : SUB * s + b0 + RUNS, :],
+                )
 
         def copy_on(vector, dst, src):
             if vector:
@@ -93,8 +97,8 @@ def tile_s2conv_pa_t_kernel(tc, x, psi, out):
             src = raw[s][:, :, CBLK * q : CBLK * (q + 1)]
             copy_on(
                 vector,
-                dst.rearrange("p (a i) r -> p a r i", i=2),
-                src.rearrange("p r (a i) -> p a r i", i=2),
+                dst.rearrange("p (a i) r -> p a r i", i=4),
+                src.rearrange("p r (a i) -> p a r i", i=4),
             )
 
         def quantise(k, q):
@@ -145,13 +149,16 @@ def tile_s2conv_pa_t_kernel(tc, x, psi, out):
                     nc.scalar.mul(out=dst, in_=src, mul=SCALE)
 
         def store(h, y):
-            nc.sync.dma_start(
-                out=out[GH * y : GH * (y + 1), P * h : P * (h + 1), :].rearrange("g b n -> b g n"),
-                in_=stg[(h, y)][:],
-            )
+            for g0 in range(0, GH, RUNS):
+                nc.sync.dma_start(
+                    out=out[GH * y + g0 : GH * y + g0 + RUNS, P * h : P * (h + 1), :].rearrange("g b n -> b g n"),
+                    in_=stg[(h, y)][:, g0 : g0 + RUNS, :],
+                )
 
         praw = raw_pool.tile([P, GOUT, PACK, COEF], BF16, name="praw", tag="raw")
-        nc.sync.dma_start(out=praw[:].rearrange("p g j c -> p g (j c)"), in_=pv)
+        pt = praw[:].rearrange("p g j c -> p g (j c)")
+        for g0 in range(0, GOUT, RUNS):
+            nc.sync.dma_start(out=pt[:, g0 : g0 + RUNS, :], in_=pv[:, g0 : g0 + RUNS, :])
         for s in range(3):
             load(s)
         pgrp = grp_pool.tile([P, 2 * 4 * P, PACK], BF16, name="pgrp", tag="grp", align_bytes=64)

@@ -1,9 +1,7 @@
 import math
 from contextlib import ExitStack
 
-import concourse.bass as bass
 import concourse.mybir as mybir
-import concourse.tile as tile
 
 FP8X4 = mybir.dt.float8_e4m3fn_x4
 BF16 = mybir.dt.bfloat16
@@ -13,34 +11,44 @@ U8 = mybir.dt.uint8
 
 P = 128
 PACK = 4
-BATCH, FEAT, GOUT, COEF = 256, 512, 16, 64
-NDEG = 8
-OUTW = 680
-FLOPS = 2 * FEAT * BATCH * GOUT * OUTW
-SCALE = 1.0 / math.sqrt(FEAT)
+BATCH, FEATURES, G_OUT, COEFS = 256, 512, 16, 64
+DEGREES = 8
+OUT_COLS = 680
+FLOPS = 2 * FEATURES * BATCH * G_OUT * OUT_COLS
+SCALE = 1.0 / math.sqrt(FEATURES)
 
-RUNS = 4
-SUB = 16
-NSUB = BATCH // SUB
-CHUNK = 64
-SUBS_PER_CHUNK = CHUNK // SUB
-CBLK = 16
-NCBLK = COEF // CBLK
-GH = 8
-BANK_C = 4
-NBANK = COEF // BANK_C
+LOAD_ROWS = 16
+LOADS = BATCH // LOAD_ROWS
+LOADS_AHEAD = 3
+CHUNK_ROWS = 64
+LOADS_PER_CHUNK = CHUNK_ROWS // LOAD_ROWS
+CHUNKS_PER_HALF = P // CHUNK_ROWS
+TILE_COEFS = 16
+COEF_TILES = COEFS // TILE_COEFS
+G_HALF = 8
+WINDOWS = DEGREES // 2
+BANK_PASSES = 4
+BANKS = COEFS // BANK_PASSES
+BANKS_PER_TILE = BANKS // COEF_TILES
 
-DEGREE = [l for l in range(NDEG) for u in range(2 * l + 1)]
-ORDER_U = [u for l in range(NDEG) for u in range(2 * l + 1)]
-BLOCK0 = [sum((2 * k + 1) ** 2 for k in range(l)) for l in range(NDEG)]
-WINDOW = [l if l < 4 else 7 - l for l in range(NDEG)]
-WOFF = [GH * (2 * (7 - l) + 1) if l < 4 else 0 for l in range(NDEG)]
+BANKS_PER_LOAD = 5
+SPLIT_BANK = 14
+
+DEGREE_OF = [l for l in range(DEGREES) for u in range(2 * l + 1)]
+FIRST_COL = [
+    sum((2 * k + 1) ** 2 for k in range(l)) + u * (2 * l + 1) for l in range(DEGREES) for u in range(2 * l + 1)
+]
+WINDOW_OF = [min(l, DEGREES - 1 - l) for l in range(DEGREES)]
+WINDOW_START = [G_HALF * (2 * (DEGREES - 1 - l) + 1) if l < WINDOWS else 0 for l in range(DEGREES)]
+
+assert len(DEGREE_OF) == COEFS and FIRST_COL[-1] + 2 * DEGREES - 1 == OUT_COLS
+assert (4 * FIRST_COL[BANK_PASSES * SPLIT_BANK]) % 32 == 0 and (4 * OUT_COLS) % 32 == 0
 
 
-def degree_runs(i):
+def degree_runs(first_coef):
     runs = []
-    for t in range(BANK_C):
-        l = DEGREE[BANK_C * i + t]
+    for t in range(BANK_PASSES):
+        l = DEGREE_OF[first_coef + t]
         if runs and runs[-1][0] == l:
             runs[-1][2] += 1
         else:
@@ -50,173 +58,153 @@ def degree_runs(i):
 
 def tile_s2conv_pa_t_kernel(tc, x, psi, out):
     nc = tc.nc
-    xv = x.rearrange("b (p j) c -> p b (j c)", j=PACK)
-    pv = psi.rearrange("g (p j) c -> p g (j c)", j=PACK)
+    x_runs = x.rearrange("b (p j) c -> p b (j c)", j=PACK)
+    psi_runs = psi.rearrange("g (p j) c -> p g (j c)", j=PACK)
 
     with ExitStack() as ctx:
-        raw_pool = ctx.enter_context(tc.tile_pool(name="raw", bufs=4))
-        grp_pool = ctx.enter_context(tc.tile_pool(name="grp", bufs=6))
-        cod_pool = ctx.enter_context(tc.tile_pool(name="cod", bufs=6))
-        stg_pool = ctx.enter_context(tc.tile_pool(name="stg", bufs=4))
-        psi_pool = ctx.enter_context(tc.tile_pool(name="psi", bufs=1))
+        raw_pool = ctx.enter_context(tc.tile_pool(name="raw", bufs=LOADS_AHEAD + 1))
+        grouped_pool = ctx.enter_context(tc.tile_pool(name="grouped", bufs=COEF_TILES + 2))
+        words_pool = ctx.enter_context(tc.tile_pool(name="words", bufs=COEF_TILES + 2))
+        staging_pool = ctx.enter_context(tc.tile_pool(name="staging", bufs=4))
+        filter_pool = ctx.enter_context(tc.tile_pool(name="filter", bufs=1))
         psum = ctx.enter_context(tc.psum_pool(name="psum", bufs=8))
         ctx.enter_context(tc.manual_schedule())
 
         raw = {}
-        grp = {}
-        cod = {}
-        scl = {}
-        stg = {}
+        grouped = {}
+        words = {}
+        planes = {}
+        staging = {}
 
-        def load(s):
-            t = raw_pool.tile([P, SUB * PACK, COEF], BF16, name="raw%d" % s, tag="raw")
-            raw[s] = t
-            tv = t[:].rearrange("p (b j) c -> p b (j c)", j=PACK)
-            for b0 in range(0, SUB, RUNS):
-                queue = nc.sync if (b0 // RUNS) % 2 == 0 else nc.scalar
-                queue.dma_start(
-                    out=tv[:, b0 : b0 + RUNS, :],
-                    in_=xv[:, SUB * s + b0 : SUB * s + b0 + RUNS, :],
-                )
-
-        def copy_on(vector, dst, src):
-            if vector:
+        def copy(on_vector, dst, src):
+            if on_vector:
                 nc.vector.tensor_copy(out=dst, in_=src)
             else:
                 nc.scalar.copy(out=dst, in_=src)
 
-        def regroup(s, q, vector):
-            k = s // SUBS_PER_CHUNK
-            part = s % SUBS_PER_CHUNK
-            if part == 0:
-                grp[(k, q)] = grp_pool.tile(
-                    [P, CBLK, CHUNK * PACK], BF16, name="grp%d_%d" % (k, q), tag="grp", align_bytes=64
-                )
-            width = SUB * PACK
-            dst = grp[(k, q)][:, :, width * part : width * (part + 1)]
-            src = raw[s][:, :, CBLK * q : CBLK * (q + 1)]
-            copy_on(
-                vector,
-                dst.rearrange("p (a i) r -> p a r i", i=4),
-                src.rearrange("p r (a i) -> p a r i", i=4),
+        def load(n):
+            raw[n] = raw_pool.tile([P, LOAD_ROWS * PACK, COEFS], BF16, name="raw%d" % n, tag="raw")
+            nc.sync.dma_start(
+                out=raw[n][:].rearrange("p (b j) c -> p b (j c)", j=PACK),
+                in_=x_runs[:, LOAD_ROWS * n : LOAD_ROWS * (n + 1), :],
             )
 
-        def quantise(k, q):
-            h = k // 2
-            half = k % 2
-            if half == 0:
-                cod[(h, q)] = cod_pool.tile(
-                    [P, CBLK, P], U32, name="cod%d_%d" % (h, q), tag="cod", align_bytes=64
+        def regroup(n, q, on_vector):
+            chunk, part = divmod(n, LOADS_PER_CHUNK)
+            if part == 0:
+                grouped[(chunk, q)] = grouped_pool.tile(
+                    [P, TILE_COEFS, CHUNK_ROWS * PACK], BF16, name="grouped%d_%d" % (chunk, q), tag="grouped",
+                    align_bytes=64,
                 )
-                scl[(h, q)] = cod_pool.tile(
-                    [P, CBLK, P], U8, name="scl%d_%d" % (h, q), tag="scl", align_bytes=64
+            width = LOAD_ROWS * PACK
+            copy(
+                on_vector,
+                grouped[(chunk, q)][:, :, width * part : width * (part + 1)].rearrange("p (a i) r -> p a r i", i=4),
+                raw[n][:, :, TILE_COEFS * q : TILE_COEFS * (q + 1)].rearrange("p r (a i) -> p a r i", i=4),
+            )
+
+        def quantise(chunk, q):
+            half, part = divmod(chunk, CHUNKS_PER_HALF)
+            if part == 0:
+                words[(half, q)] = words_pool.tile(
+                    [P, TILE_COEFS, P], U32, name="words%d_%d" % (half, q), tag="words", align_bytes=64
                 )
-            cols = slice(CHUNK * half, CHUNK * (half + 1))
-            for c in range(CBLK):
+                planes[(half, q)] = words_pool.tile(
+                    [P, TILE_COEFS, P], U8, name="planes%d_%d" % (half, q), tag="planes", align_bytes=64
+                )
+            rows = slice(CHUNK_ROWS * part, CHUNK_ROWS * (part + 1))
+            for c in range(TILE_COEFS):
                 nc.vector.quantize_mx(
-                    out=cod[(h, q)][:, c, cols].bitcast(FP8X4),
-                    scales=scl[(h, q)][:, c, cols],
-                    in_=grp[(k, q)][:, c, :],
+                    out=words[(half, q)][:, c, rows].bitcast(FP8X4),
+                    scales=planes[(half, q)][:, c, rows],
+                    in_=grouped[(chunk, q)][:, c, :],
                 )
 
-        def bank(h, y, i, vector):
-            if (h, y) not in stg:
-                stg[(h, y)] = stg_pool.tile([P, GH, OUTW], F32, name="stg%d_%d" % (h, y), tag="stg")
-            acc = psum.tile([P, BANK_C, P], F32, name="acc%d_%d_%d" % (h, y, i), tag="acc")
-            q = i // (NBANK // NCBLK)
-            for t in range(BANK_C):
-                c = BANK_C * i + t
-                w = P * (4 * y + WINDOW[DEGREE[c]])
+        def multiply_bank(half, y, i, on_vector):
+            if (half, y) not in staging:
+                staging[(half, y)] = staging_pool.tile(
+                    [P, G_HALF, OUT_COLS], F32, name="staging%d_%d" % (half, y), tag="staging"
+                )
+            bank = psum.tile([P, BANK_PASSES, P], F32, name="bank%d_%d_%d" % (half, y, i), tag="bank")
+            q = i // BANKS_PER_TILE
+            for t in range(BANK_PASSES):
+                coef = BANK_PASSES * i + t
+                w = P * (WINDOWS * y + WINDOW_OF[DEGREE_OF[coef]])
                 nc.tensor.matmul_mx(
-                    out=acc[:, t, :],
-                    lhsT=cod[(h, q)][:, c % CBLK, :].bitcast(FP8X4),
-                    lhsT_scale=scl[(h, q)][:, c % CBLK, :],
-                    rhs=pcod[:, w : w + P].bitcast(FP8X4),
-                    rhs_scale=pscl[:, w : w + P],
+                    out=bank[:, t, :],
+                    lhsT=words[(half, q)][:, coef % TILE_COEFS, :].bitcast(FP8X4),
+                    lhsT_scale=planes[(half, q)][:, coef % TILE_COEFS, :],
+                    rhs=filter_words[:, w : w + P].bitcast(FP8X4),
+                    rhs_scale=filter_planes[:, w : w + P],
                     start=True,
                     stop=True,
                 )
-            for l, t0, n in degree_runs(i):
+            for l, t0, n in degree_runs(BANK_PASSES * i):
                 d = 2 * l + 1
-                col = BLOCK0[l] + ORDER_U[BANK_C * i + t0] * d
-                src = acc[:, t0 : t0 + n, WOFF[l] : WOFF[l] + GH * d].rearrange(
-                    "p n (g m) -> p g n m", g=GH
-                )
-                dst = stg[(h, y)][:, :, col : col + n * d].rearrange("p g (n m) -> p g n m", n=n)
-                if vector:
+                col = FIRST_COL[BANK_PASSES * i + t0]
+                src = bank[:, t0 : t0 + n, WINDOW_START[l] : WINDOW_START[l] + G_HALF * d]
+                src = src.rearrange("p n (g m) -> p g n m", g=G_HALF)
+                dst = staging[(half, y)][:, :, col : col + n * d].rearrange("p g (n m) -> p g n m", n=n)
+                if on_vector:
                     nc.vector.tensor_scalar_mul(out=dst, in0=src, scalar1=SCALE)
                 else:
                     nc.scalar.mul(out=dst, in_=src, mul=SCALE)
 
-        def store(h, y):
-            for g0 in range(0, GH, RUNS):
-                nc.sync.dma_start(
-                    out=out[GH * y + g0 : GH * y + g0 + RUNS, P * h : P * (h + 1), :].rearrange("g b n -> b g n"),
-                    in_=stg[(h, y)][:, g0 : g0 + RUNS, :],
-                )
+        def store(half, y):
+            nc.sync.dma_start(
+                out=out[G_HALF * y : G_HALF * (y + 1), P * half : P * (half + 1), :].rearrange("g b n -> b g n"),
+                in_=staging[(half, y)][:],
+            )
 
-        praw = raw_pool.tile([P, GOUT, PACK, COEF], BF16, name="praw", tag="raw")
-        pt = praw[:].rearrange("p g j c -> p g (j c)")
-        for g0 in range(0, GOUT, RUNS):
-            nc.sync.dma_start(out=pt[:, g0 : g0 + RUNS, :], in_=pv[:, g0 : g0 + RUNS, :])
-        for s in range(3):
-            load(s)
-        pgrp = grp_pool.tile([P, 2 * 4 * P, PACK], BF16, name="pgrp", tag="grp", align_bytes=64)
-        pcod = psi_pool.tile([P, 2 * 4 * P], U32, name="pcod", align_bytes=64)
-        pscl = psi_pool.tile([P, 2 * 4 * P], U8, name="pscl", align_bytes=64)
+        filter_raw = raw_pool.tile([P, G_OUT, PACK, COEFS], BF16, name="filter_raw", tag="raw")
+        nc.sync.dma_start(out=filter_raw[:].rearrange("p g j c -> p g (j c)"), in_=psi_runs)
+        for n in range(LOADS_AHEAD):
+            load(n)
+        filter_grouped = grouped_pool.tile(
+            [P, 2 * WINDOWS * P, PACK], BF16, name="filter_grouped", tag="grouped", align_bytes=64
+        )
+        filter_words = filter_pool.tile([P, 2 * WINDOWS * P], U32, name="filter_words", align_bytes=64)
+        filter_planes = filter_pool.tile([P, 2 * WINDOWS * P], U8, name="filter_planes", align_bytes=64)
         for y in range(2):
-            for l in range(NDEG):
+            for l in range(DEGREES):
                 d = 2 * l + 1
-                c0 = P * (4 * y + WINDOW[l]) + WOFF[l]
-                copy_on(
+                first = P * (WINDOWS * y + WINDOW_OF[l]) + WINDOW_START[l]
+                copy(
                     y == 0,
-                    pgrp[:, c0 : c0 + GH * d, :].rearrange("p (g m) j -> p g m j", g=GH),
-                    praw[:, GH * y : GH * (y + 1), :, l * l : l * l + d].rearrange("p g j m -> p g m j"),
+                    filter_grouped[:, first : first + G_HALF * d, :].rearrange("p (g m) j -> p g m j", g=G_HALF),
+                    filter_raw[:, G_HALF * y : G_HALF * (y + 1), :, l * l : l * l + d].rearrange("p g j m -> p g m j"),
                 )
 
-        todo = [(0, y, i) for y in range(2) for i in range(NBANK)]
-        done = 0
-        for s in range(NSUB):
-            if s + 3 < NSUB:
-                load(s + 3)
-            k = s // SUBS_PER_CHUNK
-            part = s % SUBS_PER_CHUNK
-            nvec = 2 if s < 8 else 3
-            for q in range(NCBLK):
-                regroup(s, q, q < nvec)
-            if s >= 8:
-                for n in range(4 if s < 10 else 5):
-                    if done < len(todo):
-                        h, y, i = todo[done]
-                        bank(h, y, i, False)
-                        done += 1
-            if s == 0:
+        first_half_banks = [(y, i) for y in range(2) for i in range(BANKS)]
+        emptied = 0
+        for n in range(LOADS):
+            if n + LOADS_AHEAD < LOADS:
+                load(n + LOADS_AHEAD)
+            chunk, part = divmod(n, LOADS_PER_CHUNK)
+            vector_tiles = 3 if LOADS // 2 <= n < LOADS - 1 else 2
+            for q in range(COEF_TILES):
+                regroup(n, q, q < vector_tiles)
+            if n >= LOADS // 2:
+                for y, i in first_half_banks[emptied : emptied + BANKS_PER_LOAD]:
+                    multiply_bank(0, y, i, False)
+                emptied += BANKS_PER_LOAD
+            if n == 0:
                 nc.vector.quantize_mx(
-                    out=pcod[:].bitcast(FP8X4),
-                    scales=pscl[:],
-                    in_=pgrp[:].rearrange("p n j -> p (n j)"),
+                    out=filter_words[:].bitcast(FP8X4),
+                    scales=filter_planes[:],
+                    in_=filter_grouped[:].rearrange("p n j -> p (n j)"),
                 )
-            if s == NSUB - 1:
-                for q in range(NCBLK):
-                    quantise(k, q)
-            elif part == 3:
-                quantise(k, 0)
-                quantise(k, 1)
-            elif part == 0 and k > 0:
-                quantise(k - 1, 2)
-            elif part == 1 and k > 0:
-                quantise(k - 1, 3)
-        for h, y, i in todo[done:]:
-            bank(h, y, i, False)
+            if n == LOADS - 1:
+                for q in range(COEF_TILES):
+                    quantise(chunk, q)
+            elif part == LOADS_PER_CHUNK - 1:
+                quantise(chunk, 0)
+                quantise(chunk, 1)
+            elif chunk > 0 and part < 2:
+                quantise(chunk - 1, 2 + part)
         store(0, 0)
         store(0, 1)
-        for i in range(NBANK):
-            bank(1, 0, i, i >= 14)
-        store(1, 0)
-        vlist = list(range(5, 14))
-        slist = [0, 1, 2, 3, 4, 14, 15]
-        for n in range(len(vlist)):
-            bank(1, 1, vlist[n], True)
-            if n < len(slist):
-                bank(1, 1, slist[n], False)
-        store(1, 1)
+        for y in range(2):
+            for i in range(BANKS):
+                multiply_bank(1, y, i, (i < SPLIT_BANK) == (y == 1))
+            store(1, y)

@@ -65,10 +65,9 @@ def tile_s2conv_pa_t_kernel(tc, x, psi, out):
         raw_pool = ctx.enter_context(tc.tile_pool(name="raw", bufs=LOADS_AHEAD + 1))
         grouped_pool = ctx.enter_context(tc.tile_pool(name="grouped", bufs=COEF_TILES + 2))
         words_pool = ctx.enter_context(tc.tile_pool(name="words", bufs=COEF_TILES + 2))
-        staging_pool = ctx.enter_context(tc.tile_pool(name="staging", bufs=4))
+        staging_pool = ctx.enter_context(tc.tile_pool(name="staging", bufs=2 * 2))
         filter_pool = ctx.enter_context(tc.tile_pool(name="filter", bufs=1))
         psum = ctx.enter_context(tc.psum_pool(name="psum", bufs=8))
-        ctx.enter_context(tc.manual_schedule())
 
         raw = {}
         grouped = {}
@@ -99,20 +98,20 @@ def tile_s2conv_pa_t_kernel(tc, x, psi, out):
             width = LOAD_ROWS * PACK
             copy(
                 on_vector,
-                grouped[(chunk, q)][:, :, width * part : width * (part + 1)].rearrange("p (a i) r -> p a r i", i=4),
-                raw[n][:, :, TILE_COEFS * q : TILE_COEFS * (q + 1)].rearrange("p r (a i) -> p a r i", i=4),
+                grouped[(chunk, q)][:, :, width * part : width * (part + 1)].rearrange("p (a e) r -> p a r e", e=4),
+                raw[n][:, :, TILE_COEFS * q : TILE_COEFS * (q + 1)].rearrange("p r (a e) -> p a r e", e=4),
             )
 
         def quantise(chunk, q):
-            half, part = divmod(chunk, CHUNKS_PER_HALF)
-            if part == 0:
+            half, side = divmod(chunk, CHUNKS_PER_HALF)
+            if side == 0:
                 words[(half, q)] = words_pool.tile(
                     [P, TILE_COEFS, P], U32, name="words%d_%d" % (half, q), tag="words", align_bytes=64
                 )
                 planes[(half, q)] = words_pool.tile(
                     [P, TILE_COEFS, P], U8, name="planes%d_%d" % (half, q), tag="planes", align_bytes=64
                 )
-            rows = slice(CHUNK_ROWS * part, CHUNK_ROWS * (part + 1))
+            rows = slice(CHUNK_ROWS * side, CHUNK_ROWS * (side + 1))
             for c in range(TILE_COEFS):
                 nc.vector.quantize_mx(
                     out=words[(half, q)][:, c, rows].bitcast(FP8X4),
@@ -139,12 +138,12 @@ def tile_s2conv_pa_t_kernel(tc, x, psi, out):
                     start=True,
                     stop=True,
                 )
-            for l, t0, n in degree_runs(BANK_PASSES * i):
+            for l, t0, count in degree_runs(BANK_PASSES * i):
                 d = 2 * l + 1
                 col = FIRST_COL[BANK_PASSES * i + t0]
-                src = bank[:, t0 : t0 + n, WINDOW_START[l] : WINDOW_START[l] + G_HALF * d]
-                src = src.rearrange("p n (g m) -> p g n m", g=G_HALF)
-                dst = staging[(half, y)][:, :, col : col + n * d].rearrange("p g (n m) -> p g n m", n=n)
+                src = bank[:, t0 : t0 + count, WINDOW_START[l] : WINDOW_START[l] + G_HALF * d]
+                src = src.rearrange("p u (g m) -> p g u m", g=G_HALF)
+                dst = staging[(half, y)][:, :, col : col + count * d].rearrange("p g (u m) -> p g u m", u=count)
                 if on_vector:
                     nc.vector.tensor_scalar_mul(out=dst, in0=src, scalar1=SCALE)
                 else:
@@ -152,7 +151,7 @@ def tile_s2conv_pa_t_kernel(tc, x, psi, out):
 
         def store(half, y):
             nc.sync.dma_start(
-                out=out[G_HALF * y : G_HALF * (y + 1), P * half : P * (half + 1), :].rearrange("g b n -> b g n"),
+                out=out[G_HALF * y : G_HALF * (y + 1), P * half : P * (half + 1), :].rearrange("g b col -> b g col"),
                 in_=staging[(half, y)][:],
             )
 
@@ -192,7 +191,7 @@ def tile_s2conv_pa_t_kernel(tc, x, psi, out):
                 nc.vector.quantize_mx(
                     out=filter_words[:].bitcast(FP8X4),
                     scales=filter_planes[:],
-                    in_=filter_grouped[:].rearrange("p n j -> p (n j)"),
+                    in_=filter_grouped[:].rearrange("p w j -> p (w j)"),
                 )
             if n == LOADS - 1:
                 for q in range(COEF_TILES):

@@ -14,6 +14,7 @@ PACK = 4
 BATCH, FEATURES, G_OUT, COEFS = 256, 512, 16, 64
 DEGREES = 8
 OUT_COLS = 680
+STAGING_COLS = 704
 FLOPS = 2 * FEATURES * BATCH * G_OUT * OUT_COLS
 SCALE = 1.0 / math.sqrt(FEATURES)
 
@@ -82,7 +83,7 @@ def tile_s2conv_pa_t_kernel(tc, x, psi, out):
                 nc.scalar.copy(out=dst, in_=src)
 
         def load(n):
-            raw[n] = raw_pool.tile([P, LOAD_ROWS * PACK, COEFS], BF16, name="raw%d" % n, tag="raw")
+            raw[n] = raw_pool.tile([P, LOAD_ROWS * PACK, COEFS], BF16, name="raw%d" % n, tag="raw", align_bytes=256)
             nc.sync.dma_start(
                 out=raw[n][:].rearrange("p (b j) c -> p b (j c)", j=PACK),
                 in_=x_runs[:, LOAD_ROWS * n : LOAD_ROWS * (n + 1), :],
@@ -122,7 +123,7 @@ def tile_s2conv_pa_t_kernel(tc, x, psi, out):
         def multiply_bank(half, y, i, on_vector):
             if (half, y) not in staging:
                 staging[(half, y)] = staging_pool.tile(
-                    [P, G_HALF, OUT_COLS], F32, name="staging%d_%d" % (half, y), tag="staging"
+                    [P, G_HALF, STAGING_COLS], F32, name="staging%d_%d" % (half, y), tag="staging", align_bytes=256
                 )
             bank = psum.tile([P, BANK_PASSES, P], F32, name="bank%d_%d_%d" % (half, y, i), tag="bank")
             q = i // BANKS_PER_TILE
@@ -152,10 +153,10 @@ def tile_s2conv_pa_t_kernel(tc, x, psi, out):
         def store(half, y):
             nc.sync.dma_start(
                 out=out[G_HALF * y : G_HALF * (y + 1), P * half : P * (half + 1), :].rearrange("g b col -> b g col"),
-                in_=staging[(half, y)][:],
+                in_=staging[(half, y)][:, :, 0:OUT_COLS],
             )
 
-        filter_raw = raw_pool.tile([P, G_OUT, PACK, COEFS], BF16, name="filter_raw", tag="raw")
+        filter_raw = raw_pool.tile([P, G_OUT, PACK, COEFS], BF16, name="filter_raw", tag="raw", align_bytes=256)
         nc.sync.dma_start(out=filter_raw[:].rearrange("p g j c -> p g (j c)"), in_=psi_runs)
         for n in range(LOADS_AHEAD):
             load(n)

@@ -85,7 +85,7 @@ def tile_s2conv_pa_t_kernel(tc, x, psi, out):
         def load(n):
             raw[n] = raw_pool.tile([P, LOAD_ROWS * PACK, COEFS], BF16, name="raw%d" % n, tag="raw", align_bytes=256)
             nc.sync.dma_start(
-                out=raw[n][:].rearrange("p (b j) c -> p b (j c)", j=PACK),
+                out=raw[n][:].rearrange("p r c -> p (r c)"),
                 in_=x_runs[:, LOAD_ROWS * n : LOAD_ROWS * (n + 1), :],
             )
 

import math
from contextlib import ExitStack

import concourse.mybir as mybir

FP8X4 = mybir.dt.float8_e4m3fn_x4
BF16 = mybir.dt.bfloat16
F32 = mybir.dt.float32
U32 = mybir.dt.uint32
U8 = mybir.dt.uint8

P = 128
PACK = 4
BATCH, FEATURES, G_OUT, COEFS = 256, 512, 16, 64
DEGREES = 8
OUT_COLS = 680
STAGING_COLS = 704
FLOPS = 2 * FEATURES * BATCH * G_OUT * OUT_COLS
SCALE = 1.0 / math.sqrt(FEATURES)

LOAD_ROWS = 16
LOADS = BATCH // LOAD_ROWS
LOADS_AHEAD = 3
CHUNK_ROWS = 64
LOADS_PER_CHUNK = CHUNK_ROWS // LOAD_ROWS
CHUNKS_PER_HALF = P // CHUNK_ROWS
TILE_COEFS = 16
COEF_TILES = COEFS // TILE_COEFS
G_HALF = 8
WINDOWS = DEGREES // 2
BANK_PASSES = 4
BANKS = COEFS // BANK_PASSES
BANKS_PER_TILE = BANKS // COEF_TILES

BANKS_PER_LOAD = 5
SPLIT_BANK = 14

DEGREE_OF = [l for l in range(DEGREES) for u in range(2 * l + 1)]
FIRST_COL = [
    sum((2 * k + 1) ** 2 for k in range(l)) + u * (2 * l + 1) for l in range(DEGREES) for u in range(2 * l + 1)
]
WINDOW_OF = [min(l, DEGREES - 1 - l) for l in range(DEGREES)]
WINDOW_START = [G_HALF * (2 * (DEGREES - 1 - l) + 1) if l < WINDOWS else 0 for l in range(DEGREES)]

assert len(DEGREE_OF) == COEFS and FIRST_COL[-1] + 2 * DEGREES - 1 == OUT_COLS
assert (4 * FIRST_COL[BANK_PASSES * SPLIT_BANK]) % 32 == 0 and (4 * OUT_COLS) % 32 == 0


def degree_runs(first_coef):
    runs = []
    for t in range(BANK_PASSES):
        l = DEGREE_OF[first_coef + t]
        if runs and runs[-1][0] == l:
            runs[-1][2] += 1
        else:
            runs.append([l, t, 1])
    return runs


def tile_s2conv_pa_t_kernel(tc, x, psi, out):
    nc = tc.nc
    x_runs = x.rearrange("b (p j) c -> p b (j c)", j=PACK)
    psi_runs = psi.rearrange("g (p j) c -> p g (j c)", j=PACK)

    with ExitStack() as ctx:
        raw_pool = ctx.enter_context(tc.tile_pool(name="raw", bufs=LOADS_AHEAD + 1))
        grouped_pool = ctx.enter_context(tc.tile_pool(name="grouped", bufs=COEF_TILES + 2))
        words_pool = ctx.enter_context(tc.tile_pool(name="words", bufs=COEF_TILES + 2))
        staging_pool = ctx.enter_context(tc.tile_pool(name="staging", bufs=2 * 2))
        filter_pool = ctx.enter_context(tc.tile_pool(name="filter", bufs=1))
        psum = ctx.enter_context(tc.psum_pool(name="psum", bufs=8))

        raw = {}
        grouped = {}
        words = {}
        planes = {}
        staging = {}

        def copy(on_vector, dst, src):
            if on_vector:
                nc.vector.tensor_copy(out=dst, in_=src)
            else:
                nc.scalar.copy(out=dst, in_=src)

        def load(n):
            raw[n] = raw_pool.tile([P, LOAD_ROWS * PACK, COEFS], BF16, name="raw%d" % n, tag="raw", align_bytes=256)
            nc.sync.dma_start(
                out=raw[n][:].rearrange("p r c -> p (r c)"),
                in_=x_runs[:, LOAD_ROWS * n : LOAD_ROWS * (n + 1), :],
            )

        def regroup(n, q, on_vector):
            chunk, part = divmod(n, LOADS_PER_CHUNK)
            if part == 0:
                grouped[(chunk, q)] = grouped_pool.tile(
                    [P, TILE_COEFS, CHUNK_ROWS * PACK], BF16, name="grouped%d_%d" % (chunk, q), tag="grouped",
                    align_bytes=64,
                )
            width = LOAD_ROWS * PACK
            copy(
                on_vector,
                grouped[(chunk, q)][:, :, width * part : width * (part + 1)].rearrange("p (a e) r -> p a r e", e=4),
                raw[n][:, :, TILE_COEFS * q : TILE_COEFS * (q + 1)].rearrange("p r (a e) -> p a r e", e=4),
            )

        def quantise(chunk, q):
            half, side = divmod(chunk, CHUNKS_PER_HALF)
            if side == 0:
                words[(half, q)] = words_pool.tile(
                    [P, TILE_COEFS, P], U32, name="words%d_%d" % (half, q), tag="words", align_bytes=64
                )
                planes[(half, q)] = words_pool.tile(
                    [P, TILE_COEFS, P], U8, name="planes%d_%d" % (half, q), tag="planes", align_bytes=64
                )
            rows = slice(CHUNK_ROWS * side, CHUNK_ROWS * (side + 1))
            for c in range(TILE_COEFS):
                nc.vector.quantize_mx(
                    out=words[(half, q)][:, c, rows].bitcast(FP8X4),
                    scales=planes[(half, q)][:, c, rows],
                    in_=grouped[(chunk, q)][:, c, :],
                )

        def multiply_bank(half, y, i, on_vector):
            if (half, y) not in staging:
                staging[(half, y)] = staging_pool.tile(
                    [P, G_HALF, STAGING_COLS], F32, name="staging%d_%d" % (half, y), tag="staging", align_bytes=256
                )
            bank = psum.tile([P, BANK_PASSES, P], F32, name="bank%d_%d_%d" % (half, y, i), tag="bank")
            q = i // BANKS_PER_TILE
            for t in range(BANK_PASSES):
                coef = BANK_PASSES * i + t
                w = P * (WINDOWS * y + WINDOW_OF[DEGREE_OF[coef]])
                nc.tensor.matmul_mx(
                    out=bank[:, t, :],
                    lhsT=words[(half, q)][:, coef % TILE_COEFS, :].bitcast(FP8X4),
                    lhsT_scale=planes[(half, q)][:, coef % TILE_COEFS, :],
                    rhs=filter_words[:, w : w + P].bitcast(FP8X4),
                    rhs_scale=filter_planes[:, w : w + P],
                    start=True,
                    stop=True,
                )
            for l, t0, count in degree_runs(BANK_PASSES * i):
                d = 2 * l + 1
                col = FIRST_COL[BANK_PASSES * i + t0]
                src = bank[:, t0 : t0 + count, WINDOW_START[l] : WINDOW_START[l] + G_HALF * d]
                src = src.rearrange("p u (g m) -> p g u m", g=G_HALF)
                dst = staging[(half, y)][:, :, col : col + count * d].rearrange("p g (u m) -> p g u m", u=count)
                if on_vector:
                    nc.vector.tensor_scalar_mul(out=dst, in0=src, scalar1=SCALE)
                else:
                    nc.scalar.mul(out=dst, in_=src, mul=SCALE)

        def store(half, y):
            nc.sync.dma_start(
                out=out[G_HALF * y : G_HALF * (y + 1), P * half : P * (half + 1), :].rearrange("g b col -> b g col"),
                in_=staging[(half, y)][:, :, 0:OUT_COLS],
            )

        filter_raw = raw_pool.tile([P, G_OUT, PACK, COEFS], BF16, name="filter_raw", tag="raw", align_bytes=256)
        nc.sync.dma_start(out=filter_raw[:].rearrange("p g j c -> p g (j c)"), in_=psi_runs)
        for n in range(LOADS_AHEAD):
            load(n)
        filter_grouped = grouped_pool.tile(
            [P, 2 * WINDOWS * P, PACK], BF16, name="filter_grouped", tag="grouped", align_bytes=64
        )
        filter_words = filter_pool.tile([P, 2 * WINDOWS * P], U32, name="filter_words", align_bytes=64)
        filter_planes = filter_pool.tile([P, 2 * WINDOWS * P], U8, name="filter_planes", align_bytes=64)
        for y in range(2):
            for l in range(DEGREES):
                d = 2 * l + 1
                first = P * (WINDOWS * y + WINDOW_OF[l]) + WINDOW_START[l]
                copy(
                    y == 0,
                    filter_grouped[:, first : first + G_HALF * d, :].rearrange("p (g m) j -> p g m j", g=G_HALF),
                    filter_raw[:, G_HALF * y : G_HALF * (y + 1), :, l * l : l * l + d].rearrange("p g j m -> p g m j"),
                )

        first_half_banks = [(y, i) for y in range(2) for i in range(BANKS)]
        emptied = 0
        for n in range(LOADS):
            if n + LOADS_AHEAD < LOADS:
                load(n + LOADS_AHEAD)
            chunk, part = divmod(n, LOADS_PER_CHUNK)
            vector_tiles = 3 if LOADS // 2 <= n < LOADS - 1 else 2
            for q in range(COEF_TILES):
                regroup(n, q, q < vector_tiles)
            if n >= LOADS // 2:
                for y, i in first_half_banks[emptied : emptied + BANKS_PER_LOAD]:
                    multiply_bank(0, y, i, False)
                emptied += BANKS_PER_LOAD
            if n == 0:
                nc.vector.quantize_mx(
                    out=filter_words[:].bitcast(FP8X4),
                    scales=filter_planes[:],
                    in_=filter_grouped[:].rearrange("p w j -> p (w j)"),
                )
            if n == LOADS - 1:
                for q in range(COEF_TILES):
                    quantise(chunk, q)
            elif part == LOADS_PER_CHUNK - 1:
                quantise(chunk, 0)
                quantise(chunk, 1)
            elif chunk > 0 and part < 2:
                quantise(chunk - 1, 2 + part)
        store(0, 0)
        store(0, 1)
        for y in range(2):
            for i in range(BANKS):
                multiply_bank(1, y, i, (i < SPLIT_BANK) == (y == 1))
            store(1, y)
